import numpy as np
import ml_dtypes


def mxq(x, axis, fmt="e4m3"):
    dtype, down = {"e4m3": (ml_dtypes.float8_e4m3fn, 7), "e5m2": (ml_dtypes.float8_e5m2, 14)}[fmt]
    v = np.moveaxis(np.asarray(x, np.float32).astype(ml_dtypes.bfloat16).astype(np.float64), axis, -1)
    blocks = v.reshape(v.shape[:-1] + (-1, 32))
    amax = np.abs(blocks).max(-1, keepdims=True)
    byte = np.maximum(np.where(amax > 0, np.frexp(amax)[1] - 1 + 127, 0) - down, 1)
    scale = np.exp2(byte - 127.0)
    codes = (blocks / scale).astype(np.float32).astype(dtype).astype(np.float64)
    return np.moveaxis((codes * scale).reshape(v.shape), -1, axis)


WIDE = False


def mx_kscale(k):
    if not WIDE:
        return np.ones(k)
    levels = np.array([10, -10, 5, -5, 0])
    a = np.random.permutation(np.resize(levels, k // 512 * 4)).reshape(k // 512, 4)
    idx = np.arange(k)
    return np.exp2(a[idx // 512, idx % 128 // 32])


BF16 = ml_dtypes.bfloat16


def bf(x):
    return np.asarray(x, np.float32).astype(BF16)


def f64(x):
    return np.asarray(x).astype(np.float64)


E2M1 = np.array([0.0, 0.5, 1.0, 1.5, 2.0, 3.0, 4.0, 6.0, -0.0, -0.5, -1.0, -1.5, -2.0, -3.0, -4.0, -6.0])


def pack_weight(w, fmt):
    k, n = w.shape
    w = f64(bf(w)).reshape(k // 32, 32, n)
    amax = np.abs(w).max(1)
    if fmt == "e4m3":
        byte = np.frexp(amax)[1] - 1 + 127 - 7
    else:
        mant, ex = np.frexp(amax / 6.0)
        byte = np.where(mant > 0.5, ex, ex - 1) + 127
    byte = np.clip(np.where(amax > 0, byte, 1), 1, 254)
    scaled = (w * np.exp2(127.0 - byte)[:, None, :]).reshape(k, n).astype(np.float32)
    by_word = np.ascontiguousarray(scaled.reshape(k // 512, 128, 4, n).transpose(0, 1, 3, 2))
    if fmt == "e4m3":
        words = by_word.astype(ml_dtypes.float8_e4m3fn).view(np.uint8)
    else:
        c = by_word.astype(ml_dtypes.float4_e2m1fn).view(np.uint8) & 0xF
        words = c[..., 0::2] | (c[..., 1::2] << 4)
    return np.ascontiguousarray(words), np.ascontiguousarray(byte.astype(np.uint8).reshape(k // 512, 16, n))


def unpack_weight(words, scales, fmt):
    g, p, n, _ = words.shape
    if fmt == "e4m3":
        vals = np.ascontiguousarray(words).view(ml_dtypes.float8_e4m3fn).astype(np.float64)
    else:
        nib = np.empty((g, p, n, 4), np.uint8)
        nib[..., 0::2] = words & 0xF
        nib[..., 1::2] = words >> 4
        vals = E2M1[nib]
    vals = vals * np.repeat(np.exp2(scales.astype(np.float64) - 127.0), 8, axis=1)[..., None]
    return vals.transpose(0, 1, 3, 2).reshape(g * 512, n)


B, M, N, P = 2, 16384, 512, 256
EPS = 1e-05


def normalize(v, axes, gamma, beta):
    mean = v.mean(axis=axes, keepdims=True)
    std = np.sqrt(v.var(axis=axes, keepdims=True, ddof=1))
    return gamma * ((v - mean) / (std + EPS)) + beta


def setup_inputs():
    s = mx_kscale(M)
    x = bf(np.random.standard_normal((B, M, N)) * s[:, None])
    xj_words, xj_scales = pack_weight(np.random.standard_normal((M, P)) * 0.5 / np.sqrt(M) / s[:, None], "e4m3")
    xi_words, xi_scales = pack_weight(np.random.standard_normal((N, P)) * 2.0 / np.sqrt(N), "e4m3")
    return {"x": x,
            "permuted_xj_y_words": xj_words,
            "permuted_xj_y_scales": xj_scales,
            "permuted_xi_y_words": xi_words,
            "permuted_xi_y_scales": xi_scales,
            "gamma_p_sum": bf(1.0 + 0.1 * np.random.standard_normal(P)),
            "gamma_p": bf(1.0 + 0.1 * np.random.standard_normal((P, P))),
            "beta_p_sum": bf(0.1 * np.random.standard_normal(P)),
            "beta_p": bf(0.1 * np.random.standard_normal((P, P)))}


def reference(x, permuted_xj_y_words, permuted_xj_y_scales, permuted_xi_y_words, permuted_xi_y_scales, gamma_p_sum, gamma_p, beta_p_sum, beta_p):
    permuted = np.swapaxes(f64(x), -1, -2)
    pyy = mxq(permuted, 2, "e4m3") @ unpack_weight(permuted_xj_y_words, permuted_xj_y_scales, "e4m3")
    p_sum = normalize(pyy.sum(axis=-2), (-1,), f64(gamma_p_sum), f64(beta_p_sum)) + 1.0
    pyy = mxq(np.swapaxes(pyy, -1, -2), 2, "e4m3") @ unpack_weight(permuted_xi_y_words, permuted_xi_y_scales, "e4m3")
    pyy = np.swapaxes(pyy, -1, -2)
    pyy = normalize(pyy, (-2, -1), f64(gamma_p), f64(beta_p))
    return pyy, p_sum

@@ -1,0 +1,295 @@
+from contextlib import ExitStack
+
+import concourse.mybir as mybir
+from concourse.masks import make_identity
+
+F32 = mybir.dt.float32
+BF16 = mybir.dt.bfloat16
+I32 = mybir.dt.int32
+U32 = mybir.dt.uint32
+U8 = mybir.dt.uint8
+FP8X4 = mybir.dt.float8_e4m3fn_x4
+ACT = mybir.ActivationFunctionType
+ALU = mybir.AluOpType
+
+P = 128
+PACK = 4
+K_PASS = P * PACK
+B, M, N, J = 2, 16384, 512, 256
+PASSES = M // K_PASS
+J_TILES = J // P
+EPS = 1e-5
+FLOPS = 2 * B * M * N * J + 2 * B * N * J * J
+
+WEIGHT_GROUP = 4
+RAW_BUFS = 12
+RUN = 4
+
+
+def tile_selfprojection_pb_k_kernel(
+    tc,
+    x,
+    xj_words,
+    xj_scales,
+    xi_words,
+    xi_scales,
+    gamma_p_sum,
+    gamma_p,
+    beta_p_sum,
+    beta_p,
+    out_0,
+    out_1,
+):
+    nc = tc.nc
+    with ExitStack() as ctx:
+        ctx.enter_context(tc.manual_schedule())
+        keep = ctx.enter_context(tc.tile_pool(name="keep", bufs=1))
+        raw_pool = ctx.enter_context(tc.tile_pool(name="raw", bufs=RAW_BUFS))
+        work = ctx.enter_context(tc.tile_pool(name="work", bufs=3))
+        psum = ctx.enter_context(tc.psum_pool(name="psum", bufs=1))
+
+        wj_planes = keep.tile([P, PASSES, J], U8, align_bytes=64)
+        nc.vector.memset(wj_planes[:].bitcast(I32), 0)
+        wi_plane = keep.tile([P, J], U8, align_bytes=64)
+        nc.vector.memset(wi_plane[:].bitcast(I32), 0)
+        c_cols = [keep.tile([P, P], F32, name="c_cols%d" % jt) for jt in range(J_TILES)]
+        for jt in range(J_TILES):
+            nc.vector.memset(c_cols[jt][:], 0.0)
+        ones = keep.tile([P, P], F32)
+        nc.vector.memset(ones[:], 1.0)
+        warm = keep.tile([P, 1], F32)
+        nc.scalar.activation(out=warm[:], in_=ones[:, 0:1], func=ACT.Sqrt)
+        ident_bf = keep.tile([P, P], BF16)
+        make_identity(nc, ident_bf[:])
+        ident_f32 = keep.tile([P, P], F32)
+        make_identity(nc, ident_f32[:])
+
+        wj_codes = keep.tile([P, PASSES, J], U32, align_bytes=64)
+
+        def load_weight_group(first_pass):
+            passes = slice(first_pass, first_pass + WEIGHT_GROUP)
+            nc.sync.dma_start(
+                out=wj_codes[:, passes, :].bitcast(I32),
+                in_=xj_words[passes].rearrange("g p n t -> p g (n t)").bitcast(I32),
+            )
+
+        load_weight_group(0)
+        xj_scale_rows = xj_scales.rearrange("g (Q r) n -> r Q g n", r=PACK)
+        for r in range(PACK):
+            nc.sync.dma_start(
+                out=wj_planes[r:P:32, :, :].bitcast(I32), in_=xj_scale_rows[r].bitcast(I32)
+            )
+
+        y_ps = [
+            [psum.tile([P, N], F32, name="y_ps%d%d" % (b, jt)) for jt in range(J_TILES)]
+            for b in range(B)
+        ]
+        x_chunks = x.rearrange("b (g p t) n -> b g p (t n)", p=P, t=PACK)
+        regroup_copy = [nc.scalar.copy, nc.vector.tensor_copy]
+
+        for g in range(PASSES):
+            grouped = []
+            for b in range(B):
+                raw = raw_pool.tile([P, PACK * N], BF16)
+                nc.sync.dma_start(out=raw[:], in_=x_chunks[b, g])
+                grouped_b = work.tile([P, N, PACK], BF16, align_bytes=64, name="grouped%d" % b)
+                regroup_copy[b](
+                    out=grouped_b[:].rearrange("p (c i) t -> p c t i", i=RUN),
+                    in_=raw[:].rearrange("p (t c i) -> p c t i", t=PACK, i=RUN),
+                )
+                grouped.append(grouped_b)
+            if g % WEIGHT_GROUP == 0 and g + WEIGHT_GROUP < PASSES:
+                load_weight_group(g + WEIGHT_GROUP)
+            for b in range(B):
+                x_codes = work.tile([P, N], U32, align_bytes=64, name="x_codes%d" % b)
+                x_plane = work.tile([P, N], U8, align_bytes=64, name="x_plane%d" % b)
+                nc.vector.quantize_mx(
+                    out=x_codes[:].bitcast(FP8X4),
+                    scales=x_plane[:],
+                    in_=grouped[b][:].rearrange("p n t -> p (n t)"),
+                )
+                for jt in range(J_TILES):
+                    j_cols = slice(jt * P, (jt + 1) * P)
+                    nc.tensor.matmul_mx(
+                        out=y_ps[b][jt][:],
+                        lhsT=wj_codes[:, g, j_cols].bitcast(FP8X4),
+                        lhsT_scale=wj_planes[:, g, j_cols],
+                        rhs=x_codes[:].bitcast(FP8X4),
+                        rhs_scale=x_plane[:],
+                        start=(g == 0),
+                        stop=(g == PASSES - 1),
+                    )
+
+        wi_codes = keep.tile([P, J], U32, align_bytes=64)
+        nc.sync.dma_start(
+            out=wi_codes[:].bitcast(I32),
+            in_=xi_words[0].rearrange("p n t -> p (n t)").bitcast(I32),
+        )
+        xi_scale_rows = xi_scales[0].rearrange("(Q r) n -> r Q n", r=PACK)
+        for r in range(PACK):
+            nc.sync.dma_start(
+                out=wi_plane[r:P:32, :].bitcast(I32), in_=xi_scale_rows[r].bitcast(I32)
+            )
+        gamma_sb = keep.tile([P, J_TILES, J], BF16)
+        nc.sync.dma_start(out=gamma_sb[:], in_=gamma_p.rearrange("(it p) j -> p it j", p=P))
+        beta_sb = keep.tile([P, J_TILES, J], BF16)
+        nc.sync.dma_start(out=beta_sb[:], in_=beta_p.rearrange("(it p) j -> p it j", p=P))
+        gamma_rows = keep.tile([B, J], BF16)
+        nc.sync.dma_start(out=gamma_rows[:], in_=gamma_p_sum.partition_broadcast(B))
+        beta_rows = keep.tile([B, J], BF16)
+        nc.sync.dma_start(out=beta_rows[:], in_=beta_p_sum.partition_broadcast(B))
+
+        y_bf = keep.tile([P, B, J_TILES, PACK, P], BF16)
+        yT_ps = [psum.tile([P, PACK, J], BF16, name="yT_ps%d" % b) for b in range(B)]
+        for b in range(B):
+            nc.scalar.activation(
+                out=y_bf[:, b, 0],
+                in_=y_ps[b][0][:].rearrange("p (c t) -> p t c", t=PACK),
+                func=ACT.Copy,
+                accum_out=c_cols[0][:, b : b + 1],
+            )
+            nc.vector.tensor_scalar(
+                out=y_bf[:, b, 1],
+                in0=y_ps[b][1][:].rearrange("p (c t) -> p t c", t=PACK),
+                scalar1=1.0,
+                scalar2=None,
+                op0=ALU.mult,
+                op1=ALU.add,
+                accum_out=c_cols[1][:, b : b + 1],
+            )
+            for jt in range(J_TILES):
+                for t in range(PACK):
+                    nc.tensor.transpose(
+                        out=yT_ps[b][:, t, jt * P : (jt + 1) * P],
+                        in_=y_bf[:, b, jt, t, :],
+                        identity=ident_bf[:],
+                    )
+
+        c_rows = psum.tile([P, J], F32, tag="y_ps00")
+        for jt in range(J_TILES):
+            nc.tensor.transpose(
+                out=c_rows[:, jt * P : (jt + 1) * P], in_=c_cols[jt][:], identity=ident_f32[:]
+            )
+
+        y_grouped = keep.tile([P, B, J, PACK], BF16, align_bytes=64)
+        nc.vector.tensor_copy(out=y_grouped[:, 0], in_=yT_ps[0][:].rearrange("p t j -> p j t"))
+        nc.scalar.copy(out=y_grouped[:, 1], in_=yT_ps[1][:].rearrange("p t j -> p j t"))
+        y_codes = keep.tile([P, B, J], U32, align_bytes=64)
+        y_plane = keep.tile([P, B, J], U8, align_bytes=64)
+        z_ps = [psum.tile([P, J_TILES, J], F32, name="z_ps%d" % b) for b in range(B)]
+        for b in range(B):
+            nc.vector.quantize_mx(
+                out=y_codes[:, b, :].bitcast(FP8X4),
+                scales=y_plane[:, b, :],
+                in_=y_grouped[:, b].rearrange("p j t -> p (j t)"),
+            )
+            for it in range(J_TILES):
+                i_cols = slice(it * P, (it + 1) * P)
+                nc.tensor.matmul_mx(
+                    out=z_ps[b][:, it, :],
+                    lhsT=wi_codes[:, i_cols].bitcast(FP8X4),
+                    lhsT_scale=wi_plane[:, i_cols],
+                    rhs=y_codes[:, b, :].bitcast(FP8X4),
+                    rhs_scale=y_plane[:, b, :],
+                    start=True,
+                    stop=True,
+                )
+
+        c_stats = keep.tile([B, 6], F32)
+        nc.vector.bn_stats(out=c_stats[:], in_=c_rows[0:B, :])
+        c_mv = keep.tile([B, 2], F32)
+        nc.vector.bn_aggr(out=c_mv[:], in_=c_stats[:])
+        c_gained = keep.tile([B, J], F32)
+        nc.vector.scalar_tensor_tensor(
+            out=c_gained[:],
+            in0=c_rows[0:B, :],
+            scalar=c_mv[:, 0:1],
+            in1=gamma_rows[:],
+            op0=ALU.subtract,
+            op1=ALU.mult,
+        )
+        beta_plus_1 = keep.tile([B, J], F32)
+        nc.vector.tensor_scalar_add(out=beta_plus_1[:], in0=beta_rows[:], scalar1=1.0)
+
+        z_sb = keep.tile([P, B, J_TILES * J], F32)
+        z_sum0 = keep.tile([P, 1], F32)
+        z_sum1 = keep.tile([P, 1], F32)
+        nc.scalar.activation(
+            out=z_sb[:, 0, :],
+            in_=z_ps[0][:].rearrange("p it j -> p (it j)"),
+            func=ACT.Copy,
+            accum_out=z_sum0[:],
+        )
+        nc.vector.tensor_scalar(
+            out=z_sb[:, 1, :],
+            in0=z_ps[1][:].rearrange("p it j -> p (it j)"),
+            scalar1=1.0,
+            scalar2=None,
+            op0=ALU.mult,
+            op1=ALU.add,
+            accum_out=z_sum1[:],
+        )
+        totals = psum.tile([P, 2 * B], F32, tag="y_ps10")
+        nc.tensor.matmul(out=totals[:, 0:1], lhsT=ones[:], rhs=z_sum0[:], start=True, stop=True)
+        nc.tensor.matmul(out=totals[:, 1:2], lhsT=ones[:], rhs=z_sum1[:], start=True, stop=True)
+
+        c_std = keep.tile([B, 1], F32)
+        nc.scalar.activation(out=c_std[:], in_=c_mv[:, 1:2], func=ACT.Sqrt, scale=J / (J - 1.0))
+        nc.vector.tensor_scalar_add(out=c_std[:], in0=c_std[:], scalar1=EPS)
+        c_rstd = keep.tile([B, 1], F32)
+        nc.vector.reciprocal(out=c_rstd[:], in_=c_std[:])
+        p_sum = keep.tile([B, J], F32)
+        nc.vector.scalar_tensor_tensor(
+            out=p_sum[:],
+            in0=c_gained[:],
+            scalar=c_rstd[:],
+            in1=beta_plus_1[:],
+            op0=ALU.mult,
+            op1=ALU.add,
+        )
+        nc.sync.dma_start(out=out_1, in_=p_sum[:])
+
+        count = float(J * J)
+        neg_mean = keep.tile([P, B], F32)
+        nc.vector.tensor_scalar_mul(out=neg_mean[:], in0=totals[:, 0:B], scalar1=-1.0 / count)
+        squares = keep.tile([P, J_TILES * J], F32)
+        sq_sum = keep.tile([P, B], F32)
+        z_gained = keep.tile([P, B, J_TILES * J], F32)
+        for b in range(B):
+            nc.scalar.activation(
+                out=squares[:],
+                in_=z_sb[:, b, :],
+                func=ACT.Square,
+                bias=neg_mean[:, b : b + 1],
+                accum_out=sq_sum[:, b : b + 1],
+            )
+            nc.vector.scalar_tensor_tensor(
+                out=z_gained[:, b, :],
+                in0=z_sb[:, b, :],
+                scalar=neg_mean[:, b : b + 1],
+                in1=gamma_sb[:].rearrange("p it j -> p (it j)"),
+                op0=ALU.add,
+                op1=ALU.mult,
+            )
+        nc.tensor.matmul(out=totals[:, B : 2 * B], lhsT=ones[:], rhs=sq_sum[:], start=True, stop=True)
+        z_std = keep.tile([P, B], F32)
+        nc.scalar.activation(
+            out=z_std[:], in_=totals[:, B : 2 * B], func=ACT.Sqrt, scale=1.0 / (count - 1.0)
+        )
+        nc.vector.tensor_scalar_add(out=z_std[:], in0=z_std[:], scalar1=EPS)
+        z_rstd = keep.tile([P, B], F32)
+        nc.vector.reciprocal(out=z_rstd[:], in_=z_std[:])
+        result = keep.tile([P, B, J_TILES * J], F32)
+        for b in range(B):
+            nc.vector.scalar_tensor_tensor(
+                out=result[:, b, :],
+                in0=z_gained[:, b, :],
+                scalar=z_rstd[:, b : b + 1],
+                in1=beta_sb[:].rearrange("p it j -> p (it j)"),
+                op0=ALU.mult,
+                op1=ALU.add,
+            )
+            nc.sync.dma_start(
+                out=out_0[b].rearrange("(it p) j -> p it j", p=P),
+                in_=result[:, b, :].rearrange("p (it j) -> p it j", it=J_TILES),
+            )

@@ -21,9 +21,12 @@ J_TILES = J // P
 EPS = 1e-5
 FLOPS = 2 * B * M * N * J + 2 * B * N * J * J
 
-WEIGHT_GROUP = 4
+WEIGHT_GROUP = 2
 RAW_BUFS = 12
 RUN = 4
+AHEAD = 2
+CODE_BUFS = 2 * AHEAD + 4
+LAST_VECTOR_COLS = 256
 
 
 def tile_selfprojection_pb_k_kernel(
@@ -44,36 +47,48 @@ def tile_selfprojection_pb_k_kernel(
     with ExitStack() as ctx:
         ctx.enter_context(tc.manual_schedule())
         keep = ctx.enter_context(tc.tile_pool(name="keep", bufs=1))
+        codes_pool = ctx.enter_context(tc.tile_pool(name="codes", bufs=CODE_BUFS))
         raw_pool = ctx.enter_context(tc.tile_pool(name="raw", bufs=RAW_BUFS))
         work = ctx.enter_context(tc.tile_pool(name="work", bufs=3))
         psum = ctx.enter_context(tc.psum_pool(name="psum", bufs=1))
 
-        wj_planes = keep.tile([P, PASSES, J], U8, align_bytes=64)
-        nc.vector.memset(wj_planes[:].bitcast(I32), 0)
-        wi_plane = keep.tile([P, J], U8, align_bytes=64)
-        nc.vector.memset(wi_plane[:].bitcast(I32), 0)
-        c_cols = [keep.tile([P, P], F32, name="c_cols%d" % jt) for jt in range(J_TILES)]
-        for jt in range(J_TILES):
-            nc.vector.memset(c_cols[jt][:], 0.0)
-        ones = keep.tile([P, P], F32)
-        nc.vector.memset(ones[:], 1.0)
-        warm = keep.tile([P, 1], F32)
-        nc.scalar.activation(out=warm[:], in_=ones[:, 0:1], func=ACT.Sqrt)
-        ident_bf = keep.tile([P, P], BF16)
-        make_identity(nc, ident_bf[:])
-        ident_f32 = keep.tile([P, P], F32)
-        make_identity(nc, ident_f32[:])
-
+        x_chunks = x.rearrange("b (g p t) n -> b g p (t n)", p=P, t=PACK)
         wj_codes = keep.tile([P, PASSES, J], U32, align_bytes=64)
+        wj_planes = keep.tile([P, PASSES, J], U8, align_bytes=64)
+        wi_codes = keep.tile([P, J], U32, align_bytes=64)
+        wi_plane = keep.tile([P, J], U8, align_bytes=64)
+        raw_tiles = {}
 
-        def load_weight_group(first_pass):
-            passes = slice(first_pass, first_pass + WEIGHT_GROUP)
+        def load_x(g):
+            for b in range(B):
+                raw = raw_pool.tile([P, PACK * N], BF16, name="raw")
+                nc.sync.dma_start(out=raw[:], in_=x_chunks[b, g])
+                raw_tiles[b, g] = raw
+
+        def load_weights(first_pass, count):
+            passes = slice(first_pass, first_pass + count)
             nc.sync.dma_start(
                 out=wj_codes[:, passes, :].bitcast(I32),
                 in_=xj_words[passes].rearrange("g p n t -> p g (n t)").bitcast(I32),
             )
 
-        load_weight_group(0)
+        for g in range(AHEAD):
+            load_x(g)
+
+        nc.vector.memset(wj_planes[:].bitcast(I32), 0)
+        nc.vector.memset(wi_plane[:].bitcast(I32), 0)
+        c_cols = [keep.tile([P, P], F32, name="c_cols%d" % jt) for jt in range(J_TILES)]
+        for jt in range(J_TILES):
+            nc.gpsimd.memset(c_cols[jt][:], 0.0)
+        averaging = keep.tile([P, P], F32)
+        nc.gpsimd.memset(averaging[:], 1.0 / P)
+        warm = keep.tile([P, 1], F32)
+        nc.scalar.activation(out=warm[:], in_=averaging[:, 0:1], func=ACT.Sqrt)
+        ident_bf = keep.tile([P, P], BF16)
+        make_identity(nc, ident_bf[:])
+        ident_f32 = keep.tile([P, P], F32)
+        make_identity(nc, ident_f32[:])
+
         xj_scale_rows = xj_scales.rearrange("g (Q r) n -> r Q g n", r=PACK)
         for r in range(PACK):
             nc.sync.dma_start(
@@ -84,64 +99,52 @@ def tile_selfprojection_pb_k_kernel(
             [psum.tile([P, N], F32, name="y_ps%d%d" % (b, jt)) for jt in range(J_TILES)]
             for b in range(B)
         ]
-        x_chunks = x.rearrange("b (g p t) n -> b g p (t n)", p=P, t=PACK)
-        regroup_copy = [nc.scalar.copy, nc.vector.tensor_copy]
-
-        for g in range(PASSES):
-            grouped = []
-            for b in range(B):
-                raw = raw_pool.tile([P, PACK * N], BF16)
-                nc.sync.dma_start(out=raw[:], in_=x_chunks[b, g])
-                grouped_b = work.tile([P, N, PACK], BF16, align_bytes=64, name="grouped%d" % b)
-                regroup_copy[b](
-                    out=grouped_b[:].rearrange("p (c i) t -> p c t i", i=RUN),
-                    in_=raw[:].rearrange("p (t c i) -> p c t i", t=PACK, i=RUN),
-                )
-                grouped.append(grouped_b)
-            if g % WEIGHT_GROUP == 0 and g + WEIGHT_GROUP < PASSES:
-                load_weight_group(g + WEIGHT_GROUP)
-            for b in range(B):
-                x_codes = work.tile([P, N], U32, align_bytes=64, name="x_codes%d" % b)
-                x_plane = work.tile([P, N], U8, align_bytes=64, name="x_plane%d" % b)
-                nc.vector.quantize_mx(
-                    out=x_codes[:].bitcast(FP8X4),
-                    scales=x_plane[:],
-                    in_=grouped[b][:].rearrange("p n t -> p (n t)"),
-                )
-                for jt in range(J_TILES):
-                    j_cols = slice(jt * P, (jt + 1) * P)
-                    nc.tensor.matmul_mx(
-                        out=y_ps[b][jt][:],
-                        lhsT=wj_codes[:, g, j_cols].bitcast(FP8X4),
-                        lhsT_scale=wj_planes[:, g, j_cols],
-                        rhs=x_codes[:].bitcast(FP8X4),
-                        rhs_scale=x_plane[:],
-                        start=(g == 0),
-                        stop=(g == PASSES - 1),
-                    )
-
-        wi_codes = keep.tile([P, J], U32, align_bytes=64)
-        nc.sync.dma_start(
-            out=wi_codes[:].bitcast(I32),
-            in_=xi_words[0].rearrange("p n t -> p (n t)").bitcast(I32),
-        )
-        xi_scale_rows = xi_scales[0].rearrange("(Q r) n -> r Q n", r=PACK)
-        for r in range(PACK):
-            nc.sync.dma_start(
-                out=wi_plane[r:P:32, :].bitcast(I32), in_=xi_scale_rows[r].bitcast(I32)
-            )
         gamma_sb = keep.tile([P, J_TILES, J], BF16)
-        nc.sync.dma_start(out=gamma_sb[:], in_=gamma_p.rearrange("(it p) j -> p it j", p=P))
         beta_sb = keep.tile([P, J_TILES, J], BF16)
-        nc.sync.dma_start(out=beta_sb[:], in_=beta_p.rearrange("(it p) j -> p it j", p=P))
         gamma_rows = keep.tile([B, J], BF16)
-        nc.sync.dma_start(out=gamma_rows[:], in_=gamma_p_sum.partition_broadcast(B))
         beta_rows = keep.tile([B, J], BF16)
-        nc.sync.dma_start(out=beta_rows[:], in_=beta_p_sum.partition_broadcast(B))
+        beta_plus_1 = keep.tile([B, J], F32)
+
+        def load_second_weights():
+            nc.sync.dma_start(
+                out=wi_codes[:].bitcast(I32),
+                in_=xi_words[0].rearrange("p n t -> p (n t)").bitcast(I32),
+            )
+            xi_scale_rows = xi_scales[0].rearrange("(Q r) n -> r Q n", r=PACK)
+            for r in range(PACK):
+                nc.sync.dma_start(
+                    out=wi_plane[r:P:32, :].bitcast(I32), in_=xi_scale_rows[r].bitcast(I32)
+                )
+
+        def load_gains():
+            nc.sync.dma_start(out=gamma_sb[:], in_=gamma_p.rearrange("(it p) j -> p it j", p=P))
+            nc.sync.dma_start(out=beta_sb[:], in_=beta_p.rearrange("(it p) j -> p it j", p=P))
+
+        def load_sum_gains():
+            nc.sync.dma_start(out=gamma_rows[:], in_=gamma_p_sum.partition_broadcast(B))
+            nc.sync.dma_start(out=beta_rows[:], in_=beta_p_sum.partition_broadcast(B))
+            nc.gpsimd.tensor_scalar(
+                out=beta_plus_1[:], in0=beta_rows[:], scalar1=1.0, scalar2=1.0, op0=ALU.mult, op1=ALU.add
+            )
 
         y_bf = keep.tile([P, B, J_TILES, PACK, P], BF16)
-        yT_ps = [psum.tile([P, PACK, J], BF16, name="yT_ps%d" % b) for b in range(B)]
-        for b in range(B):
+        y_grouped = keep.tile([P, B, J, PACK], BF16, align_bytes=64)
+        y_codes = keep.tile([P, B, J], U32, align_bytes=64)
+        y_plane = keep.tile([P, B, J], U8, align_bytes=64)
+        z_stats = keep.tile([P, B, 6], F32)
+        z_mv = keep.tile([P, B, 2], F32)
+        dev_sq = keep.tile([P, B], F32)
+        z_std = keep.tile([P, B], F32)
+        z_rstd = keep.tile([P, B], F32)
+        z_gained = keep.tile([P, B, J_TILES * J], F32)
+        result = keep.tile([P, B, J_TILES * J], F32)
+        yT_ps = {}
+        z_ps = {}
+        z_mean = {}
+        z_var = {}
+        count = float(J * J)
+
+        def y_leaves_psum(b):
             nc.scalar.activation(
                 out=y_bf[:, b, 0],
                 in_=y_ps[b][0][:].rearrange("p (c t) -> p t c", t=PACK),
@@ -157,48 +160,192 @@ def tile_selfprojection_pb_k_kernel(
                 op1=ALU.add,
                 accum_out=c_cols[1][:, b : b + 1],
             )
+
+        def transpose_y(b):
             for jt in range(J_TILES):
+                yT = psum.tile([P, PACK, P], BF16, name="yT", tag="y_ps%d%d" % (b, jt))
+                yT_ps[b, jt] = yT
                 for t in range(PACK):
                     nc.tensor.transpose(
-                        out=yT_ps[b][:, t, jt * P : (jt + 1) * P],
-                        in_=y_bf[:, b, jt, t, :],
-                        identity=ident_bf[:],
+                        out=yT[:, t, :], in_=y_bf[:, b, jt, t, :], identity=ident_bf[:]
                     )
 
-        c_rows = psum.tile([P, J], F32, tag="y_ps00")
+        def group_y(b):
+            for jt, copy in enumerate([nc.scalar.copy, nc.vector.tensor_copy]):
+                copy(
+                    out=y_grouped[:, b, jt * P : (jt + 1) * P, :],
+                    in_=yT_ps[b, jt][:].rearrange("p t j -> p j t"),
+                )
+
+        def second_product(b):
+            z = psum.tile([P, J_TILES, J], F32, name="z_ps%d" % b)
+            z_ps[b] = z
+            for jt in range(J_TILES):
+                j_cols = slice(jt * P, (jt + 1) * P)
+                nc.vector.quantize_mx(
+                    out=y_codes[:, b, j_cols].bitcast(FP8X4),
+                    scales=y_plane[:, b, j_cols],
+                    in_=y_grouped[:, b, j_cols].rearrange("p j t -> p (j t)"),
+                )
+                for it in range(J_TILES):
+                    i_cols = slice(it * P, (it + 1) * P)
+                    nc.tensor.matmul_mx(
+                        out=z[:, it, j_cols],
+                        lhsT=wi_codes[:, i_cols].bitcast(FP8X4),
+                        lhsT_scale=wi_plane[:, i_cols],
+                        rhs=y_codes[:, b, j_cols].bitcast(FP8X4),
+                        rhs_scale=y_plane[:, b, j_cols],
+                        start=True,
+                        stop=True,
+                    )
+
+        def z_moments(b):
+            nc.vector.bn_stats(out=z_stats[:, b], in_=z_ps[b][:].rearrange("p it j -> p (it j)"))
+            nc.vector.bn_aggr(out=z_mv[:, b], in_=z_stats[:, b])
+            mean = psum.tile([P, 1], F32, name="z_mean%d" % b, tag="y_ps%d1" % b)
+            nc.tensor.matmul(
+                out=mean[:], lhsT=averaging[:], rhs=z_mv[:, b, 0:1], start=True, stop=True
+            )
+            var = psum.tile([P, 1], F32, name="z_var%d" % b, tag="y_ps%d0" % b)
+            nc.tensor.matmul(
+                out=var[:], lhsT=averaging[:], rhs=z_mv[:, b, 1:2], start=True, stop=False
+            )
+            z_mean[b] = mean
+            z_var[b] = var
+
+        def z_minus_mean(b):
+            nc.scalar.activation(
+                out=dev_sq[:, b : b + 1],
+                in_=z_mean[b][:],
+                func=ACT.Square,
+                scale=-1.0,
+                bias=z_mv[:, b, 0:1],
+            )
+            nc.vector.scalar_tensor_tensor(
+                out=z_gained[:, b, :],
+                in0=z_ps[b][:].rearrange("p it j -> p (it j)"),
+                scalar=z_mean[b][:],
+                in1=gamma_sb[:].rearrange("p it j -> p (it j)"),
+                op0=ALU.subtract,
+                op1=ALU.mult,
+            )
+            nc.tensor.matmul(
+                out=z_var[b][:], lhsT=averaging[:], rhs=dev_sq[:, b : b + 1], start=False, stop=True
+            )
+            nc.scalar.activation(
+                out=z_std[:, b : b + 1], in_=z_var[b][:], func=ACT.Sqrt, scale=count / (count - 1.0)
+            )
+
+        def z_result(b):
+            nc.vector.tensor_scalar_add(
+                out=z_std[:, b : b + 1], in0=z_std[:, b : b + 1], scalar1=EPS
+            )
+            nc.vector.reciprocal(out=z_rstd[:, b : b + 1], in_=z_std[:, b : b + 1])
+            for it in range(J_TILES):
+                cols = slice(it * J, (it + 1) * J)
+                nc.vector.scalar_tensor_tensor(
+                    out=result[:, b, cols],
+                    in0=z_gained[:, b, cols],
+                    scalar=z_rstd[:, b : b + 1],
+                    in1=beta_sb[:, it, :],
+                    op0=ALU.mult,
+                    op1=ALU.add,
+                )
+
+        def store(b, it):
+            nc.sync.dma_start(
+                out=out_0[b, it * P : (it + 1) * P, :], in_=result[:, b, it * J : (it + 1) * J]
+            )
+
+        codes = {}
+
+        def regroup_part(copy, tile, raw, cols):
+            rows = raw[:].rearrange("p (t n) -> p t n", t=PACK)
+            copy(
+                out=tile[:, cols, :].rearrange("p (c i) t -> p c t i", i=RUN),
+                in_=rows[:, :, cols].rearrange("p t (c i) -> p c t i", i=RUN),
+            )
+
+        def regroup(b, g):
+            tile = work.tile([P, N, PACK], BF16, align_bytes=64, name="grouped%d" % b)
+            raw = raw_tiles.pop((b, g))
+            if g == PASSES - 1:
+                regroup_part(nc.vector.tensor_copy, tile, raw, slice(0, LAST_VECTOR_COLS))
+                regroup_part(nc.scalar.copy, tile, raw, slice(LAST_VECTOR_COLS, N))
+            else:
+                regroup_part([nc.scalar.copy, nc.vector.tensor_copy][b], tile, raw, slice(0, N))
+            return tile
+
+        def quantize(b, g, tile):
+            x_codes = codes_pool.tile([P, N], U32, align_bytes=64, name="x_codes")
+            x_plane = codes_pool.tile([P, N], U8, align_bytes=64, name="x_plane")
+            nc.vector.quantize_mx(
+                out=x_codes[:].bitcast(FP8X4),
+                scales=x_plane[:],
+                in_=tile[:].rearrange("p n t -> p (n t)"),
+            )
+            codes[b, g] = (x_codes, x_plane)
+
+        def multiply(g):
+            for b in range(B):
+                x_codes, x_plane = codes.pop((b, g))
+                for jt in range(J_TILES):
+                    j_cols = slice(jt * P, (jt + 1) * P)
+                    nc.tensor.matmul_mx(
+                        out=y_ps[b][jt][:],
+                        lhsT=wj_codes[:, g, j_cols].bitcast(FP8X4),
+                        lhsT_scale=wj_planes[:, g, j_cols],
+                        rhs=x_codes[:].bitcast(FP8X4),
+                        rhs_scale=x_plane[:],
+                        start=(g == 0),
+                        stop=(g == PASSES - 1),
+                    )
+
+        for g in range(PASSES):
+            if g + AHEAD < PASSES:
+                load_x(g + AHEAD)
+                if g % WEIGHT_GROUP == 0:
+                    load_weights(g, WEIGHT_GROUP)
+            if g == PASSES - AHEAD - 2:
+                load_second_weights()
+            tiles = [regroup(b, g) for b in range(B)]
+            for b in range(B):
+                quantize(b, g, tiles[b])
+            if g >= AHEAD:
+                multiply(g - AHEAD)
+        for g in range(PASSES - AHEAD, PASSES):
+            load_weights(g, 1)
+        load_gains()
+        load_sum_gains()
+        for g in range(PASSES - AHEAD, PASSES):
+            multiply(g)
+
+        y_leaves_psum(0)
+        transpose_y(0)
+        y_leaves_psum(1)
+        group_y(0)
+        transpose_y(1)
+        c_rows = psum.tile([P, J], F32, name="c_rows", tag="c_rows")
         for jt in range(J_TILES):
             nc.tensor.transpose(
                 out=c_rows[:, jt * P : (jt + 1) * P], in_=c_cols[jt][:], identity=ident_f32[:]
             )
-
-        y_grouped = keep.tile([P, B, J, PACK], BF16, align_bytes=64)
-        nc.vector.tensor_copy(out=y_grouped[:, 0], in_=yT_ps[0][:].rearrange("p t j -> p j t"))
-        nc.scalar.copy(out=y_grouped[:, 1], in_=yT_ps[1][:].rearrange("p t j -> p j t"))
-        y_codes = keep.tile([P, B, J], U32, align_bytes=64)
-        y_plane = keep.tile([P, B, J], U8, align_bytes=64)
-        z_ps = [psum.tile([P, J_TILES, J], F32, name="z_ps%d" % b) for b in range(B)]
-        for b in range(B):
-            nc.vector.quantize_mx(
-                out=y_codes[:, b, :].bitcast(FP8X4),
-                scales=y_plane[:, b, :],
-                in_=y_grouped[:, b].rearrange("p j t -> p (j t)"),
-            )
-            for it in range(J_TILES):
-                i_cols = slice(it * P, (it + 1) * P)
-                nc.tensor.matmul_mx(
-                    out=z_ps[b][:, it, :],
-                    lhsT=wi_codes[:, i_cols].bitcast(FP8X4),
-                    lhsT_scale=wi_plane[:, i_cols],
-                    rhs=y_codes[:, b, :].bitcast(FP8X4),
-                    rhs_scale=y_plane[:, b, :],
-                    start=True,
-                    stop=True,
-                )
-
+        second_product(0)
+        group_y(1)
+        second_product(1)
+        z_moments(0)
         c_stats = keep.tile([B, 6], F32)
         nc.vector.bn_stats(out=c_stats[:], in_=c_rows[0:B, :])
         c_mv = keep.tile([B, 2], F32)
         nc.vector.bn_aggr(out=c_mv[:], in_=c_stats[:])
+        z_moments(1)
+        z_minus_mean(0)
+        c_std = keep.tile([B, 1], F32)
+        nc.scalar.activation(out=c_std[:], in_=c_mv[:, 1:2], func=ACT.Sqrt, scale=J / (J - 1.0))
+        z_minus_mean(1)
+        z_result(0)
+        for it in range(J_TILES):
+            store(0, it)
         c_gained = keep.tile([B, J], F32)
         nc.vector.scalar_tensor_tensor(
             out=c_gained[:],
@@ -208,33 +355,6 @@ def tile_selfprojection_pb_k_kernel(
             op0=ALU.subtract,
             op1=ALU.mult,
         )
-        beta_plus_1 = keep.tile([B, J], F32)
-        nc.vector.tensor_scalar_add(out=beta_plus_1[:], in0=beta_rows[:], scalar1=1.0)
-
-        z_sb = keep.tile([P, B, J_TILES * J], F32)
-        z_sum0 = keep.tile([P, 1], F32)
-        z_sum1 = keep.tile([P, 1], F32)
-        nc.scalar.activation(
-            out=z_sb[:, 0, :],
-            in_=z_ps[0][:].rearrange("p it j -> p (it j)"),
-            func=ACT.Copy,
-            accum_out=z_sum0[:],
-        )
-        nc.vector.tensor_scalar(
-            out=z_sb[:, 1, :],
-            in0=z_ps[1][:].rearrange("p it j -> p (it j)"),
-            scalar1=1.0,
-            scalar2=None,
-            op0=ALU.mult,
-            op1=ALU.add,
-            accum_out=z_sum1[:],
-        )
-        totals = psum.tile([P, 2 * B], F32, tag="y_ps10")
-        nc.tensor.matmul(out=totals[:, 0:1], lhsT=ones[:], rhs=z_sum0[:], start=True, stop=True)
-        nc.tensor.matmul(out=totals[:, 1:2], lhsT=ones[:], rhs=z_sum1[:], start=True, stop=True)
-
-        c_std = keep.tile([B, 1], F32)
-        nc.scalar.activation(out=c_std[:], in_=c_mv[:, 1:2], func=ACT.Sqrt, scale=J / (J - 1.0))
         nc.vector.tensor_scalar_add(out=c_std[:], in0=c_std[:], scalar1=EPS)
         c_rstd = keep.tile([B, 1], F32)
         nc.vector.reciprocal(out=c_rstd[:], in_=c_std[:])
@@ -248,48 +368,6 @@ def tile_selfprojection_pb_k_kernel(
             op1=ALU.add,
         )
         nc.sync.dma_start(out=out_1, in_=p_sum[:])
-
-        count = float(J * J)
-        neg_mean = keep.tile([P, B], F32)
-        nc.vector.tensor_scalar_mul(out=neg_mean[:], in0=totals[:, 0:B], scalar1=-1.0 / count)
-        squares = keep.tile([P, J_TILES * J], F32)
-        sq_sum = keep.tile([P, B], F32)
-        z_gained = keep.tile([P, B, J_TILES * J], F32)
-        for b in range(B):
-            nc.scalar.activation(
-                out=squares[:],
-                in_=z_sb[:, b, :],
-                func=ACT.Square,
-                bias=neg_mean[:, b : b + 1],
-                accum_out=sq_sum[:, b : b + 1],
-            )
-            nc.vector.scalar_tensor_tensor(
-                out=z_gained[:, b, :],
-                in0=z_sb[:, b, :],
-                scalar=neg_mean[:, b : b + 1],
-                in1=gamma_sb[:].rearrange("p it j -> p (it j)"),
-                op0=ALU.add,
-                op1=ALU.mult,
-            )
-        nc.tensor.matmul(out=totals[:, B : 2 * B], lhsT=ones[:], rhs=sq_sum[:], start=True, stop=True)
-        z_std = keep.tile([P, B], F32)
-        nc.scalar.activation(
-            out=z_std[:], in_=totals[:, B : 2 * B], func=ACT.Sqrt, scale=1.0 / (count - 1.0)
-        )
-        nc.vector.tensor_scalar_add(out=z_std[:], in0=z_std[:], scalar1=EPS)
-        z_rstd = keep.tile([P, B], F32)
-        nc.vector.reciprocal(out=z_rstd[:], in_=z_std[:])
-        result = keep.tile([P, B, J_TILES * J], F32)
-        for b in range(B):
-            nc.vector.scalar_tensor_tensor(
-                out=result[:, b, :],
-                in0=z_gained[:, b, :],
-                scalar=z_rstd[:, b : b + 1],
-                in1=beta_sb[:].rearrange("p it j -> p (it j)"),
-                op0=ALU.mult,
-                op1=ALU.add,
-            )
-            nc.sync.dma_start(
-                out=out_0[b].rearrange("(it p) j -> p it j", p=P),
-                in_=result[:, b, :].rearrange("p (it j) -> p it j", it=J_TILES),
-            )
+        z_result(1)
+        for it in range(J_TILES):
+            store(1, it)

@@ -88,6 +88,15 @@ def tile_selfprojection_pb_k_kernel(
         make_identity(nc, ident_bf[:])
         ident_f32 = keep.tile([P, P], F32)
         make_identity(nc, ident_f32[:])
+        centering = keep.tile([P, P], F32)
+        nc.gpsimd.tensor_scalar(
+            out=centering[:],
+            in0=ident_f32[:],
+            scalar1=1.0,
+            scalar2=-1.0 / P,
+            op0=ALU.mult,
+            op1=ALU.add,
+        )
 
         xj_scale_rows = xj_scales.rearrange("g (Q r) n -> r Q g n", r=PACK)
         for r in range(PACK):
@@ -133,15 +142,15 @@ def tile_selfprojection_pb_k_kernel(
         y_plane = keep.tile([P, B, J], U8, align_bytes=64)
         z_stats = keep.tile([P, B, 6], F32)
         z_mv = keep.tile([P, B, 2], F32)
-        dev_sq = keep.tile([P, B], F32)
+        z_bias = keep.tile([P, 2 * B], F32)
+        dev_sq = keep.tile([P, P], F32)
+        dev_sum = keep.tile([P, B], F32)
         z_std = keep.tile([P, B], F32)
         z_rstd = keep.tile([P, B], F32)
         z_gained = keep.tile([P, B, J_TILES * J], F32)
         result = keep.tile([P, B, J_TILES * J], F32)
         yT_ps = {}
         z_ps = {}
-        z_mean = {}
-        z_var = {}
         count = float(J * J)
 
         def y_leaves_psum(b):
@@ -199,63 +208,78 @@ def tile_selfprojection_pb_k_kernel(
                         stop=True,
                     )
 
+        def z_matrix(b):
+            return z_ps[b][:].rearrange("p it j -> p (it j)")
+
         def z_moments(b):
-            nc.vector.bn_stats(out=z_stats[:, b], in_=z_ps[b][:].rearrange("p it j -> p (it j)"))
+            nc.vector.bn_stats(out=z_stats[:, b], in_=z_matrix(b))
             nc.vector.bn_aggr(out=z_mv[:, b], in_=z_stats[:, b])
-            mean = psum.tile([P, 1], F32, name="z_mean%d" % b, tag="y_ps%d1" % b)
-            nc.tensor.matmul(
-                out=mean[:], lhsT=averaging[:], rhs=z_mv[:, b, 0:1], start=True, stop=True
-            )
-            var = psum.tile([P, 1], F32, name="z_var%d" % b, tag="y_ps%d0" % b)
-            nc.tensor.matmul(
-                out=var[:], lhsT=averaging[:], rhs=z_mv[:, b, 1:2], start=True, stop=False
-            )
-            z_mean[b] = mean
-            z_var[b] = var
 
-        def z_minus_mean(b):
-            nc.scalar.activation(
-                out=dev_sq[:, b : b + 1],
-                in_=z_mean[b][:],
-                func=ACT.Square,
-                scale=-1.0,
-                bias=z_mv[:, b, 0:1],
-            )
-            nc.vector.scalar_tensor_tensor(
-                out=z_gained[:, b, :],
-                in0=z_ps[b][:].rearrange("p it j -> p (it j)"),
-                scalar=z_mean[b][:],
-                in1=gamma_sb[:].rearrange("p it j -> p (it j)"),
-                op0=ALU.subtract,
-                op1=ALU.mult,
-            )
+        def z_averages():
+            averages = psum.tile([P, 2 * B], F32, name="averages", tag="y_ps00")
             nc.tensor.matmul(
-                out=z_var[b][:], lhsT=averaging[:], rhs=dev_sq[:, b : b + 1], start=False, stop=True
+                out=averages[:],
+                lhsT=averaging[:],
+                rhs=z_mv[:].rearrange("p b m -> p (b m)"),
+                start=True,
+                stop=True,
             )
-            nc.scalar.activation(
-                out=z_std[:, b : b + 1], in_=z_var[b][:], func=ACT.Sqrt, scale=count / (count - 1.0)
-            )
+            deviations = psum.tile([P, B, P], F32, name="deviations", tag="y_ps01")
+            for b in range(B):
+                nc.tensor.matmul(
+                    out=deviations[:, b, :],
+                    lhsT=z_mv[:, b, 0:1].to_broadcast([P, P]),
+                    rhs=centering[:],
+                    start=True,
+                    stop=True,
+                )
+            return averages, deviations
 
-        def z_result(b):
-            nc.vector.tensor_scalar_add(
-                out=z_std[:, b : b + 1], in0=z_std[:, b : b + 1], scalar1=EPS
+        def z_rstds(averages, deviations):
+            unbiased = count / (count - 1.0)
+            nc.vector.tensor_scalar(
+                out=z_bias[:],
+                in0=averages[:],
+                scalar1=unbiased,
+                scalar2=None,
+                op0=ALU.mult,
             )
-            nc.vector.reciprocal(out=z_rstd[:, b : b + 1], in_=z_std[:, b : b + 1])
-            for it in range(J_TILES):
-                cols = slice(it * J, (it + 1) * J)
+            for b in range(B):
+                nc.scalar.activation(
+                    out=dev_sq[:],
+                    in_=deviations[:, b, :],
+                    func=ACT.Square,
+                    accum_out=dev_sum[:, b : b + 1],
+                )
+            for b in range(B):
+                nc.scalar.activation(
+                    out=z_std[:, b : b + 1],
+                    in_=dev_sum[:, b : b + 1],
+                    func=ACT.Sqrt,
+                    scale=unbiased / P,
+                    bias=z_bias[:, 2 * b + 1 : 2 * b + 2],
+                )
+            for b in range(B):
                 nc.vector.scalar_tensor_tensor(
-                    out=result[:, b, cols],
-                    in0=z_gained[:, b, cols],
-                    scalar=z_rstd[:, b : b + 1],
-                    in1=beta_sb[:, it, :],
-                    op0=ALU.mult,
-                    op1=ALU.add,
+                    out=z_gained[:, b, :],
+                    in0=z_matrix(b),
+                    scalar=averages[:, 2 * b : 2 * b + 1],
+                    in1=gamma_sb[:].rearrange("p it j -> p (it j)"),
+                    op0=ALU.subtract,
+                    op1=ALU.mult,
                 )
 
-        def store(b, it):
-            nc.sync.dma_start(
-                out=out_0[b, it * P : (it + 1) * P, :], in_=result[:, b, it * J : (it + 1) * J]
+        def z_result(b, it):
+            cols = slice(it * J, (it + 1) * J)
+            nc.vector.scalar_tensor_tensor(
+                out=result[:, b, cols],
+                in0=z_gained[:, b, cols],
+                scalar=z_rstd[:, b : b + 1],
+                in1=beta_sb[:, it, :],
+                op0=ALU.mult,
+                op1=ALU.add,
             )
+            nc.sync.dma_start(out=out_0[b, it * P : (it + 1) * P, :], in_=result[:, b, cols])
 
         codes = {}
 
@@ -333,19 +357,15 @@ def tile_selfprojection_pb_k_kernel(
         second_product(0)
         group_y(1)
         second_product(1)
-        z_moments(0)
         c_stats = keep.tile([B, 6], F32)
         nc.vector.bn_stats(out=c_stats[:], in_=c_rows[0:B, :])
         c_mv = keep.tile([B, 2], F32)
         nc.vector.bn_aggr(out=c_mv[:], in_=c_stats[:])
-        z_moments(1)
-        z_minus_mean(0)
         c_std = keep.tile([B, 1], F32)
         nc.scalar.activation(out=c_std[:], in_=c_mv[:, 1:2], func=ACT.Sqrt, scale=J / (J - 1.0))
-        z_minus_mean(1)
-        z_result(0)
-        for it in range(J_TILES):
-            store(0, it)
+        for b in range(B):
+            z_moments(b)
+        averages, deviations = z_averages()
         c_gained = keep.tile([B, J], F32)
         nc.vector.scalar_tensor_tensor(
             out=c_gained[:],
@@ -368,6 +388,9 @@ def tile_selfprojection_pb_k_kernel(
             op1=ALU.add,
         )
         nc.sync.dma_start(out=out_1, in_=p_sum[:])
-        z_result(1)
-        for it in range(J_TILES):
-            store(1, it)
+        z_rstds(averages, deviations)
+        nc.vector.tensor_scalar_add(out=z_std[:], in0=z_std[:], scalar1=EPS)
+        nc.vector.reciprocal(out=z_rstd[:], in_=z_std[:])
+        for b in range(B):
+            for it in range(J_TILES):
+                z_result(b, it)

@@ -53,15 +53,15 @@ def tile_selfprojection_pb_k_kernel(
         psum = ctx.enter_context(tc.psum_pool(name="psum", bufs=1))
 
         x_chunks = x.rearrange("b (g p t) n -> b g p (t n)", p=P, t=PACK)
-        wj_codes = keep.tile([P, PASSES, J], U32, align_bytes=64)
-        wj_planes = keep.tile([P, PASSES, J], U8, align_bytes=64)
-        wi_codes = keep.tile([P, J], U32, align_bytes=64)
-        wi_plane = keep.tile([P, J], U8, align_bytes=64)
+        wj_codes = keep.tile([P, PASSES, J], U32, align_bytes=256)
+        wj_planes = keep.tile([P, PASSES, J], U8, align_bytes=256)
+        wi_codes = keep.tile([P, J], U32, align_bytes=256)
+        wi_plane = keep.tile([P, J], U8, align_bytes=256)
         raw_tiles = {}
 
         def load_x(g):
             for b in range(B):
-                raw = raw_pool.tile([P, PACK * N], BF16, name="raw")
+                raw = raw_pool.tile([P, PACK * N], BF16, align_bytes=256, name="raw")
                 nc.sync.dma_start(out=raw[:], in_=x_chunks[b, g])
                 raw_tiles[b, g] = raw
 
@@ -137,9 +137,9 @@ def tile_selfprojection_pb_k_kernel(
             )
 
         y_bf = keep.tile([P, B, J_TILES, PACK, P], BF16)
-        y_grouped = keep.tile([P, B, J, PACK], BF16, align_bytes=64)
-        y_codes = keep.tile([P, B, J], U32, align_bytes=64)
-        y_plane = keep.tile([P, B, J], U8, align_bytes=64)
+        y_grouped = keep.tile([P, B, J, PACK], BF16, align_bytes=256)
+        y_codes = keep.tile([P, B, J], U32, align_bytes=256)
+        y_plane = keep.tile([P, B, J], U8, align_bytes=256)
         z_stats = keep.tile([P, B, 6], F32)
         z_mv = keep.tile([P, B, 2], F32)
         z_bias = keep.tile([P, 2 * B], F32)
@@ -291,7 +291,7 @@ def tile_selfprojection_pb_k_kernel(
             )
 
         def regroup(b, g):
-            tile = work.tile([P, N, PACK], BF16, align_bytes=64, name="grouped%d" % b)
+            tile = work.tile([P, N, PACK], BF16, align_bytes=256, name="grouped%d" % b)
             raw = raw_tiles.pop((b, g))
             if g == PASSES - 1:
                 regroup_part(nc.vector.tensor_copy, tile, raw, slice(0, LAST_VECTOR_COLS))
@@ -301,8 +301,8 @@ def tile_selfprojection_pb_k_kernel(
             return tile
 
         def quantize(b, g, tile):
-            x_codes = codes_pool.tile([P, N], U32, align_bytes=64, name="x_codes")
-            x_plane = codes_pool.tile([P, N], U8, align_bytes=64, name="x_plane")
+            x_codes = codes_pool.tile([P, N], U32, align_bytes=256, name="x_codes")
+            x_plane = codes_pool.tile([P, N], U8, align_bytes=256, name="x_plane")
             nc.vector.quantize_mx(
                 out=x_codes[:].bitcast(FP8X4),
                 scales=x_plane[:],

@@ -18,11 +18,12 @@ K_PASS = P * PACK
 B, M, N, J = 2, 16384, 512, 256
 PASSES = M // K_PASS
 J_TILES = J // P
+Z_COLS = J_TILES * J
 EPS = 1e-5
 FLOPS = 2 * B * M * N * J + 2 * B * N * J * J
 
 WEIGHT_GROUP = 2
-RAW_BUFS = 12
+RAW_BUFS = 16
 RUN = 4
 AHEAD = 2
 CODE_BUFS = 2 * AHEAD + 4
@@ -61,7 +62,7 @@ def tile_selfprojection_pb_k_kernel(
 
         def load_x(g):
             for b in range(B):
-                raw = raw_pool.tile([P, PACK * N], BF16, align_bytes=256, name="raw")
+                raw = raw_pool.tile([P, PACK * N], BF16, align_bytes=4096, name="raw")
                 nc.sync.dma_start(out=raw[:], in_=x_chunks[b, g])
                 raw_tiles[b, g] = raw
 
@@ -84,8 +85,6 @@ def tile_selfprojection_pb_k_kernel(
         nc.gpsimd.memset(averaging[:], 1.0 / P)
         warm = keep.tile([P, 1], F32)
         nc.scalar.activation(out=warm[:], in_=averaging[:, 0:1], func=ACT.Sqrt)
-        ident_bf = keep.tile([P, P], BF16)
-        make_identity(nc, ident_bf[:])
         ident_f32 = keep.tile([P, P], F32)
         make_identity(nc, ident_f32[:])
         centering = keep.tile([P, P], F32)
@@ -136,13 +135,15 @@ def tile_selfprojection_pb_k_kernel(
                 out=beta_plus_1[:], in0=beta_rows[:], scalar1=1.0, scalar2=1.0, op0=ALU.mult, op1=ALU.add
             )
 
-        y_bf = keep.tile([P, B, J_TILES, PACK, P], BF16)
+        y_bf = keep.tile([P, B, J_TILES, N], BF16, align_bytes=256)
         y_grouped = keep.tile([P, B, J, PACK], BF16, align_bytes=256)
         y_codes = keep.tile([P, B, J], U32, align_bytes=256)
         y_plane = keep.tile([P, B, J], U8, align_bytes=256)
-        z_stats = keep.tile([P, B, 6], F32)
+        z_stats = keep.tile([P, 6], F32)
+        z_sum = keep.tile([P, 1], F32)
+        z_copy = keep.tile([P, Z_COLS], F32)
         z_mv = keep.tile([P, B, 2], F32)
-        z_bias = keep.tile([P, 2 * B], F32)
+        z_bias = keep.tile([P, B], F32)
         dev_sq = keep.tile([P, P], F32)
         dev_sum = keep.tile([P, B], F32)
         z_std = keep.tile([P, B], F32)
@@ -156,13 +157,13 @@ def tile_selfprojection_pb_k_kernel(
         def y_leaves_psum(b):
             nc.scalar.activation(
                 out=y_bf[:, b, 0],
-                in_=y_ps[b][0][:].rearrange("p (c t) -> p t c", t=PACK),
+                in_=y_ps[b][0][:],
                 func=ACT.Copy,
                 accum_out=c_cols[0][:, b : b + 1],
             )
             nc.vector.tensor_scalar(
                 out=y_bf[:, b, 1],
-                in0=y_ps[b][1][:].rearrange("p (c t) -> p t c", t=PACK),
+                in0=y_ps[b][1][:],
                 scalar1=1.0,
                 scalar2=None,
                 op0=ALU.mult,
@@ -172,18 +173,22 @@ def tile_selfprojection_pb_k_kernel(
 
         def transpose_y(b):
             for jt in range(J_TILES):
-                yT = psum.tile([P, PACK, P], BF16, name="yT", tag="y_ps%d%d" % (b, jt))
+                yT = psum.tile([P, PACK // 2, P], F32, name="yT", tag="y_ps%d%d" % (b, jt))
                 yT_ps[b, jt] = yT
-                for t in range(PACK):
+                words = y_bf[:, b, jt, :].bitcast(F32)
+                for u in range(PACK // 2):
                     nc.tensor.transpose(
-                        out=yT[:, t, :], in_=y_bf[:, b, jt, t, :], identity=ident_bf[:]
+                        out=yT[:, u, :], in_=words[:, u : N // 2 : 2], identity=ident_f32[:]
                     )
 
         def group_y(b):
             for jt, copy in enumerate([nc.scalar.copy, nc.vector.tensor_copy]):
                 copy(
-                    out=y_grouped[:, b, jt * P : (jt + 1) * P, :],
-                    in_=yT_ps[b, jt][:].rearrange("p t j -> p j t"),
+                    out=y_grouped[:, b, jt * P : (jt + 1) * P, :]
+                    .rearrange("p j t -> p (j t)")
+                    .bitcast(F32)
+                    .rearrange("p (j u) -> p j u", u=PACK // 2),
+                    in_=yT_ps[b, jt][:].rearrange("p u j -> p j u"),
                 )
 
         def second_product(b):
@@ -211,9 +216,24 @@ def tile_selfprojection_pb_k_kernel(
         def z_matrix(b):
             return z_ps[b][:].rearrange("p it j -> p (it j)")
 
-        def z_moments(b):
-            nc.vector.bn_stats(out=z_stats[:, b], in_=z_matrix(b))
-            nc.vector.bn_aggr(out=z_mv[:, b], in_=z_stats[:, b])
+        def z_moments_on_scalar(b):
+            mean, deviation = z_mv[:, b, 0:1], z_mv[:, b, 1:2]
+            nc.scalar.activation(
+                out=z_copy[:], in_=z_matrix(b), func=ACT.Copy, accum_out=z_sum[:]
+            )
+            nc.scalar.activation(out=mean, in_=z_sum[:], func=ACT.Copy, scale=1.0 / Z_COLS)
+            nc.scalar.activation(
+                out=z_copy[:],
+                in_=z_matrix(b),
+                func=ACT.Square,
+                scale=-1.0,
+                bias=mean,
+                accum_out=deviation,
+            )
+
+        def z_moments_on_vector(b):
+            nc.vector.bn_stats(out=z_stats[:], in_=z_matrix(b))
+            nc.vector.bn_aggr(out=z_mv[:, b], in_=z_stats[:])
 
         def z_averages():
             averages = psum.tile([P, 2 * B], F32, name="averages", tag="y_ps00")
@@ -237,13 +257,10 @@ def tile_selfprojection_pb_k_kernel(
 
         def z_rstds(averages, deviations):
             unbiased = count / (count - 1.0)
-            nc.vector.tensor_scalar(
-                out=z_bias[:],
-                in0=averages[:],
-                scalar1=unbiased,
-                scalar2=None,
-                op0=ALU.mult,
-            )
+            for b, factor in enumerate((unbiased / Z_COLS, unbiased)):
+                nc.vector.tensor_scalar_mul(
+                    out=z_bias[:, b : b + 1], in0=averages[:, 2 * b + 1 : 2 * b + 2], scalar1=factor
+                )
             for b in range(B):
                 nc.scalar.activation(
                     out=dev_sq[:],
@@ -257,7 +274,7 @@ def tile_selfprojection_pb_k_kernel(
                     in_=dev_sum[:, b : b + 1],
                     func=ACT.Sqrt,
                     scale=unbiased / P,
-                    bias=z_bias[:, 2 * b + 1 : 2 * b + 2],
+                    bias=z_bias[:, b : b + 1],
                 )
             for b in range(B):
                 nc.vector.scalar_tensor_tensor(
@@ -269,17 +286,21 @@ def tile_selfprojection_pb_k_kernel(
                     op1=ALU.mult,
                 )
 
-        def z_result(b, it):
-            cols = slice(it * J, (it + 1) * J)
+        def z_result(b, it, tiles):
+            cols = slice(it * J, (it + tiles) * J)
             nc.vector.scalar_tensor_tensor(
                 out=result[:, b, cols],
                 in0=z_gained[:, b, cols],
                 scalar=z_rstd[:, b : b + 1],
-                in1=beta_sb[:, it, :],
+                in1=beta_sb[:].rearrange("p it j -> p (it j)")[:, cols],
                 op0=ALU.mult,
                 op1=ALU.add,
             )
-            nc.sync.dma_start(out=out_0[b, it * P : (it + 1) * P, :], in_=result[:, b, cols])
+            rows = out_0[b, it * P : (it + tiles) * P, :]
+            nc.sync.dma_start(
+                out=rows.rearrange("(it p) j -> p it j", p=P),
+                in_=result[:, b, cols].rearrange("p (it j) -> p it j", j=J),
+            )
 
         codes = {}
 
@@ -361,10 +382,10 @@ def tile_selfprojection_pb_k_kernel(
         nc.vector.bn_stats(out=c_stats[:], in_=c_rows[0:B, :])
         c_mv = keep.tile([B, 2], F32)
         nc.vector.bn_aggr(out=c_mv[:], in_=c_stats[:])
+        z_moments_on_scalar(0)
         c_std = keep.tile([B, 1], F32)
         nc.scalar.activation(out=c_std[:], in_=c_mv[:, 1:2], func=ACT.Sqrt, scale=J / (J - 1.0))
-        for b in range(B):
-            z_moments(b)
+        z_moments_on_vector(1)
         averages, deviations = z_averages()
         c_gained = keep.tile([B, J], F32)
         nc.vector.scalar_tensor_tensor(
@@ -375,6 +396,12 @@ def tile_selfprojection_pb_k_kernel(
             op0=ALU.subtract,
             op1=ALU.mult,
         )
+        z_rstds(averages, deviations)
+        nc.vector.tensor_scalar_add(out=z_std[:], in0=z_std[:], scalar1=EPS)
+        nc.vector.reciprocal(out=z_rstd[:], in_=z_std[:])
+        z_result(0, 0, J_TILES)
+        for it in range(J_TILES):
+            z_result(1, it, 1)
         nc.vector.tensor_scalar_add(out=c_std[:], in0=c_std[:], scalar1=EPS)
         c_rstd = keep.tile([B, 1], F32)
         nc.vector.reciprocal(out=c_rstd[:], in_=c_std[:])
@@ -388,9 +415,3 @@ def tile_selfprojection_pb_k_kernel(
             op1=ALU.add,
         )
         nc.sync.dma_start(out=out_1, in_=p_sum[:])
-        z_rstds(averages, deviations)
-        nc.vector.tensor_scalar_add(out=z_std[:], in0=z_std[:], scalar1=EPS)
-        nc.vector.reciprocal(out=z_rstd[:], in_=z_std[:])
-        for b in range(B):
-            for it in range(J_TILES):
-                z_result(b, it)

@@ -22,7 +22,7 @@ Z_COLS = J_TILES * J
 EPS = 1e-5
 FLOPS = 2 * B * M * N * J + 2 * B * N * J * J
 
-WEIGHT_GROUP = 2
+WEIGHT_GROUP = 1
 RAW_BUFS = 16
 RUN = 4
 AHEAD = 2
@@ -348,11 +348,9 @@ def tile_selfprojection_pb_k_kernel(
 
         for g in range(PASSES):
             if g + AHEAD < PASSES:
-                load_x(g + AHEAD)
                 if g % WEIGHT_GROUP == 0:
                     load_weights(g, WEIGHT_GROUP)
-            if g == PASSES - AHEAD - 2:
-                load_second_weights()
+                load_x(g + AHEAD)
             tiles = [regroup(b, g) for b in range(B)]
             for b in range(B):
                 quantize(b, g, tiles[b])
@@ -360,6 +358,7 @@ def tile_selfprojection_pb_k_kernel(
                 multiply(g - AHEAD)
         for g in range(PASSES - AHEAD, PASSES):
             load_weights(g, 1)
+        load_second_weights()
         load_gains()
         load_sum_gains()
         for g in range(PASSES - AHEAD, PASSES):

from contextlib import ExitStack

import concourse.mybir as mybir
from concourse.masks import make_identity

F32 = mybir.dt.float32
BF16 = mybir.dt.bfloat16
I32 = mybir.dt.int32
U32 = mybir.dt.uint32
U8 = mybir.dt.uint8
FP8X4 = mybir.dt.float8_e4m3fn_x4
ACT = mybir.ActivationFunctionType
ALU = mybir.AluOpType

P = 128
PACK = 4
K_PASS = P * PACK
B, M, N, J = 2, 16384, 512, 256
PASSES = M // K_PASS
J_TILES = J // P
Z_COLS = J_TILES * J
EPS = 1e-5
FLOPS = 2 * B * M * N * J + 2 * B * N * J * J

WEIGHT_GROUP = 1
RAW_BUFS = 16
RUN = 4
AHEAD = 2
CODE_BUFS = 2 * AHEAD + 4
LAST_VECTOR_COLS = 256


def tile_selfprojection_pb_k_kernel(
    tc,
    x,
    xj_words,
    xj_scales,
    xi_words,
    xi_scales,
    gamma_p_sum,
    gamma_p,
    beta_p_sum,
    beta_p,
    out_0,
    out_1,
):
    nc = tc.nc
    with ExitStack() as ctx:
        ctx.enter_context(tc.manual_schedule())
        keep = ctx.enter_context(tc.tile_pool(name="keep", bufs=1))
        codes_pool = ctx.enter_context(tc.tile_pool(name="codes", bufs=CODE_BUFS))
        raw_pool = ctx.enter_context(tc.tile_pool(name="raw", bufs=RAW_BUFS))
        work = ctx.enter_context(tc.tile_pool(name="work", bufs=3))
        psum = ctx.enter_context(tc.psum_pool(name="psum", bufs=1))

        x_chunks = x.rearrange("b (g p t) n -> b g p (t n)", p=P, t=PACK)
        wj_codes = keep.tile([P, PASSES, J], U32, align_bytes=256)
        wj_planes = keep.tile([P, PASSES, J], U8, align_bytes=256)
        wi_codes = keep.tile([P, J], U32, align_bytes=256)
        wi_plane = keep.tile([P, J], U8, align_bytes=256)
        raw_tiles = {}

        def load_x(g):
            for b in range(B):
                raw = raw_pool.tile([P, PACK * N], BF16, align_bytes=4096, name="raw")
                nc.sync.dma_start(out=raw[:], in_=x_chunks[b, g])
                raw_tiles[b, g] = raw

        def load_weights(first_pass, count):
            passes = slice(first_pass, first_pass + count)
            nc.sync.dma_start(
                out=wj_codes[:, passes, :].bitcast(I32),
                in_=xj_words[passes].rearrange("g p n t -> p g (n t)").bitcast(I32),
            )

        for g in range(AHEAD):
            load_x(g)

        nc.vector.memset(wj_planes[:].bitcast(I32), 0)
        nc.vector.memset(wi_plane[:].bitcast(I32), 0)
        c_cols = [keep.tile([P, P], F32, name="c_cols%d" % jt) for jt in range(J_TILES)]
        for jt in range(J_TILES):
            nc.gpsimd.memset(c_cols[jt][:], 0.0)
        averaging = keep.tile([P, P], F32)
        nc.gpsimd.memset(averaging[:], 1.0 / P)
        warm = keep.tile([P, 1], F32)
        nc.scalar.activation(out=warm[:], in_=averaging[:, 0:1], func=ACT.Sqrt)
        ident_f32 = keep.tile([P, P], F32)
        make_identity(nc, ident_f32[:])
        centering = keep.tile([P, P], F32)
        nc.gpsimd.tensor_scalar(
            out=centering[:],
            in0=ident_f32[:],
            scalar1=1.0,
            scalar2=-1.0 / P,
            op0=ALU.mult,
            op1=ALU.add,
        )

        xj_scale_rows = xj_scales.rearrange("g (Q r) n -> r Q g n", r=PACK)
        for r in range(PACK):
            nc.sync.dma_start(
                out=wj_planes[r:P:32, :, :].bitcast(I32), in_=xj_scale_rows[r].bitcast(I32)
            )

        y_ps = [
            [psum.tile([P, N], F32, name="y_ps%d%d" % (b, jt)) for jt in range(J_TILES)]
            for b in range(B)
        ]
        gamma_sb = keep.tile([P, J_TILES, J], BF16)
        beta_sb = keep.tile([P, J_TILES, J], BF16)
        gamma_rows = keep.tile([B, J], BF16)
        beta_rows = keep.tile([B, J], BF16)
        beta_plus_1 = keep.tile([B, J], F32)

        def load_second_weights():
            nc.sync.dma_start(
                out=wi_codes[:].bitcast(I32),
                in_=xi_words[0].rearrange("p n t -> p (n t)").bitcast(I32),
            )
            xi_scale_rows = xi_scales[0].rearrange("(Q r) n -> r Q n", r=PACK)
            for r in range(PACK):
                nc.sync.dma_start(
                    out=wi_plane[r:P:32, :].bitcast(I32), in_=xi_scale_rows[r].bitcast(I32)
                )

        def load_gains():
            nc.sync.dma_start(out=gamma_sb[:], in_=gamma_p.rearrange("(it p) j -> p it j", p=P))
            nc.sync.dma_start(out=beta_sb[:], in_=beta_p.rearrange("(it p) j -> p it j", p=P))

        def load_sum_gains():
            nc.sync.dma_start(out=gamma_rows[:], in_=gamma_p_sum.partition_broadcast(B))
            nc.sync.dma_start(out=beta_rows[:], in_=beta_p_sum.partition_broadcast(B))
            nc.gpsimd.tensor_scalar(
                out=beta_plus_1[:], in0=beta_rows[:], scalar1=1.0, scalar2=1.0, op0=ALU.mult, op1=ALU.add
            )

        y_bf = keep.tile([P, B, J_TILES, N], BF16, align_bytes=256)
        y_grouped = keep.tile([P, B, J, PACK], BF16, align_bytes=256)
        y_codes = keep.tile([P, B, J], U32, align_bytes=256)
        y_plane = keep.tile([P, B, J], U8, align_bytes=256)
        z_stats = keep.tile([P, 6], F32)
        z_sum = keep.tile([P, 1], F32)
        z_copy = keep.tile([P, Z_COLS], F32)
        z_mv = keep.tile([P, B, 2], F32)
        z_bias = keep.tile([P, B], F32)
        dev_sq = keep.tile([P, P], F32)
        dev_sum = keep.tile([P, B], F32)
        z_std = keep.tile([P, B], F32)
        z_rstd = keep.tile([P, B], F32)
        z_gained = keep.tile([P, B, J_TILES * J], F32)
        result = keep.tile([P, B, J_TILES * J], F32)
        yT_ps = {}
        z_ps = {}
        count = float(J * J)

        def y_leaves_psum(b):
            nc.scalar.activation(
                out=y_bf[:, b, 0],
                in_=y_ps[b][0][:],
                func=ACT.Copy,
                accum_out=c_cols[0][:, b : b + 1],
            )
            nc.vector.tensor_scalar(
                out=y_bf[:, b, 1],
                in0=y_ps[b][1][:],
                scalar1=1.0,
                scalar2=None,
                op0=ALU.mult,
                op1=ALU.add,
                accum_out=c_cols[1][:, b : b + 1],
            )

        def transpose_y(b):
            for jt in range(J_TILES):
                yT = psum.tile([P, PACK // 2, P], F32, name="yT", tag="y_ps%d%d" % (b, jt))
                yT_ps[b, jt] = yT
                words = y_bf[:, b, jt, :].bitcast(F32)
                for u in range(PACK // 2):
                    nc.tensor.transpose(
                        out=yT[:, u, :], in_=words[:, u : N // 2 : 2], identity=ident_f32[:]
                    )

        def group_y(b):
            for jt, copy in enumerate([nc.scalar.copy, nc.vector.tensor_copy]):
                copy(
                    out=y_grouped[:, b, jt * P : (jt + 1) * P, :]
                    .rearrange("p j t -> p (j t)")
                    .bitcast(F32)
                    .rearrange("p (j u) -> p j u", u=PACK // 2),
                    in_=yT_ps[b, jt][:].rearrange("p u j -> p j u"),
                )

        def second_product(b):
            z = psum.tile([P, J_TILES, J], F32, name="z_ps%d" % b)
            z_ps[b] = z
            for jt in range(J_TILES):
                j_cols = slice(jt * P, (jt + 1) * P)
                nc.vector.quantize_mx(
                    out=y_codes[:, b, j_cols].bitcast(FP8X4),
                    scales=y_plane[:, b, j_cols],
                    in_=y_grouped[:, b, j_cols].rearrange("p j t -> p (j t)"),
                )
                for it in range(J_TILES):
                    i_cols = slice(it * P, (it + 1) * P)
                    nc.tensor.matmul_mx(
                        out=z[:, it, j_cols],
                        lhsT=wi_codes[:, i_cols].bitcast(FP8X4),
                        lhsT_scale=wi_plane[:, i_cols],
                        rhs=y_codes[:, b, j_cols].bitcast(FP8X4),
                        rhs_scale=y_plane[:, b, j_cols],
                        start=True,
                        stop=True,
                    )

        def z_matrix(b):
            return z_ps[b][:].rearrange("p it j -> p (it j)")

        def z_moments_on_scalar(b):
            mean, deviation = z_mv[:, b, 0:1], z_mv[:, b, 1:2]
            nc.scalar.activation(
                out=z_copy[:], in_=z_matrix(b), func=ACT.Copy, accum_out=z_sum[:]
            )
            nc.scalar.activation(out=mean, in_=z_sum[:], func=ACT.Copy, scale=1.0 / Z_COLS)
            nc.scalar.activation(
                out=z_copy[:],
                in_=z_matrix(b),
                func=ACT.Square,
                scale=-1.0,
                bias=mean,
                accum_out=deviation,
            )

        def z_moments_on_vector(b):
            nc.vector.bn_stats(out=z_stats[:], in_=z_matrix(b))
            nc.vector.bn_aggr(out=z_mv[:, b], in_=z_stats[:])

        def z_averages():
            averages = psum.tile([P, 2 * B], F32, name="averages", tag="y_ps00")
            nc.tensor.matmul(
                out=averages[:],
                lhsT=averaging[:],
                rhs=z_mv[:].rearrange("p b m -> p (b m)"),
                start=True,
                stop=True,
            )
            deviations = psum.tile([P, B, P], F32, name="deviations", tag="y_ps01")
            for b in range(B):
                nc.tensor.matmul(
                    out=deviations[:, b, :],
                    lhsT=z_mv[:, b, 0:1].to_broadcast([P, P]),
                    rhs=centering[:],
                    start=True,
                    stop=True,
                )
            return averages, deviations

        def z_rstds(averages, deviations):
            unbiased = count / (count - 1.0)
            for b, factor in enumerate((unbiased / Z_COLS, unbiased)):
                nc.vector.tensor_scalar_mul(
                    out=z_bias[:, b : b + 1], in0=averages[:, 2 * b + 1 : 2 * b + 2], scalar1=factor
                )
            for b in range(B):
                nc.scalar.activation(
                    out=dev_sq[:],
                    in_=deviations[:, b, :],
                    func=ACT.Square,
                    accum_out=dev_sum[:, b : b + 1],
                )
            for b in range(B):
                nc.scalar.activation(
                    out=z_std[:, b : b + 1],
                    in_=dev_sum[:, b : b + 1],
                    func=ACT.Sqrt,
                    scale=unbiased / P,
                    bias=z_bias[:, b : b + 1],
                )
            for b in range(B):
                nc.vector.scalar_tensor_tensor(
                    out=z_gained[:, b, :],
                    in0=z_matrix(b),
                    scalar=averages[:, 2 * b : 2 * b + 1],
                    in1=gamma_sb[:].rearrange("p it j -> p (it j)"),
                    op0=ALU.subtract,
                    op1=ALU.mult,
                )

        def z_result(b, it, tiles):
            cols = slice(it * J, (it + tiles) * J)
            nc.vector.scalar_tensor_tensor(
                out=result[:, b, cols],
                in0=z_gained[:, b, cols],
                scalar=z_rstd[:, b : b + 1],
                in1=beta_sb[:].rearrange("p it j -> p (it j)")[:, cols],
                op0=ALU.mult,
                op1=ALU.add,
            )
            rows = out_0[b, it * P : (it + tiles) * P, :]
            nc.sync.dma_start(
                out=rows.rearrange("(it p) j -> p it j", p=P),
                in_=result[:, b, cols].rearrange("p (it j) -> p it j", j=J),
            )

        codes = {}

        def regroup_part(copy, tile, raw, cols):
            rows = raw[:].rearrange("p (t n) -> p t n", t=PACK)
            copy(
                out=tile[:, cols, :].rearrange("p (c i) t -> p c t i", i=RUN),
                in_=rows[:, :, cols].rearrange("p t (c i) -> p c t i", i=RUN),
            )

        def regroup(b, g):
            tile = work.tile([P, N, PACK], BF16, align_bytes=256, name="grouped%d" % b)
            raw = raw_tiles.pop((b, g))
            if g == PASSES - 1:
                regroup_part(nc.vector.tensor_copy, tile, raw, slice(0, LAST_VECTOR_COLS))
                regroup_part(nc.scalar.copy, tile, raw, slice(LAST_VECTOR_COLS, N))
            else:
                regroup_part([nc.scalar.copy, nc.vector.tensor_copy][b], tile, raw, slice(0, N))
            return tile

        def quantize(b, g, tile):
            x_codes = codes_pool.tile([P, N], U32, align_bytes=256, name="x_codes")
            x_plane = codes_pool.tile([P, N], U8, align_bytes=256, name="x_plane")
            nc.vector.quantize_mx(
                out=x_codes[:].bitcast(FP8X4),
                scales=x_plane[:],
                in_=tile[:].rearrange("p n t -> p (n t)"),
            )
            codes[b, g] = (x_codes, x_plane)

        def multiply(g):
            for b in range(B):
                x_codes, x_plane = codes.pop((b, g))
                for jt in range(J_TILES):
                    j_cols = slice(jt * P, (jt + 1) * P)
                    nc.tensor.matmul_mx(
                        out=y_ps[b][jt][:],
                        lhsT=wj_codes[:, g, j_cols].bitcast(FP8X4),
                        lhsT_scale=wj_planes[:, g, j_cols],
                        rhs=x_codes[:].bitcast(FP8X4),
                        rhs_scale=x_plane[:],
                        start=(g == 0),
                        stop=(g == PASSES - 1),
                    )

        for g in range(PASSES):
            if g + AHEAD < PASSES:
                if g % WEIGHT_GROUP == 0:
                    load_weights(g, WEIGHT_GROUP)
                load_x(g + AHEAD)
            tiles = [regroup(b, g) for b in range(B)]
            for b in range(B):
                quantize(b, g, tiles[b])
            if g >= AHEAD:
                multiply(g - AHEAD)
        for g in range(PASSES - AHEAD, PASSES):
            load_weights(g, 1)
        load_second_weights()
        load_gains()
        load_sum_gains()
        for g in range(PASSES - AHEAD, PASSES):
            multiply(g)

        y_leaves_psum(0)
        transpose_y(0)
        y_leaves_psum(1)
        group_y(0)
        transpose_y(1)
        c_rows = psum.tile([P, J], F32, name="c_rows", tag="c_rows")
        for jt in range(J_TILES):
            nc.tensor.transpose(
                out=c_rows[:, jt * P : (jt + 1) * P], in_=c_cols[jt][:], identity=ident_f32[:]
            )
        second_product(0)
        group_y(1)
        second_product(1)
        c_stats = keep.tile([B, 6], F32)
        nc.vector.bn_stats(out=c_stats[:], in_=c_rows[0:B, :])
        c_mv = keep.tile([B, 2], F32)
        nc.vector.bn_aggr(out=c_mv[:], in_=c_stats[:])
        z_moments_on_scalar(0)
        c_std = keep.tile([B, 1], F32)
        nc.scalar.activation(out=c_std[:], in_=c_mv[:, 1:2], func=ACT.Sqrt, scale=J / (J - 1.0))
        z_moments_on_vector(1)
        averages, deviations = z_averages()
        c_gained = keep.tile([B, J], F32)
        nc.vector.scalar_tensor_tensor(
            out=c_gained[:],
            in0=c_rows[0:B, :],
            scalar=c_mv[:, 0:1],
            in1=gamma_rows[:],
            op0=ALU.subtract,
            op1=ALU.mult,
        )
        z_rstds(averages, deviations)
        nc.vector.tensor_scalar_add(out=z_std[:], in0=z_std[:], scalar1=EPS)
        nc.vector.reciprocal(out=z_rstd[:], in_=z_std[:])
        z_result(0, 0, J_TILES)
        for it in range(J_TILES):
            z_result(1, it, 1)
        nc.vector.tensor_scalar_add(out=c_std[:], in0=c_std[:], scalar1=EPS)
        c_rstd = keep.tile([B, 1], F32)
        nc.vector.reciprocal(out=c_rstd[:], in_=c_std[:])
        p_sum = keep.tile([B, J], F32)
        nc.vector.scalar_tensor_tensor(
            out=p_sum[:],
            in0=c_gained[:],
            scalar=c_rstd[:],
            in1=beta_plus_1[:],
            op0=ALU.mult,
            op1=ALU.add,
        )
        nc.sync.dma_start(out=out_1, in_=p_sum[:])
